import numpy as np
import ml_dtypes

BF16 = ml_dtypes.bfloat16


def bf(x):
    return np.asarray(x, np.float32).astype(BF16)


def f32(x):
    return np.asarray(x, np.float32)


def f64(x):
    return np.asarray(x).astype(np.float64)


def striped(idx):
    return np.tile(idx.reshape(-1, 16).T, (8, 1))


K, D, DH, F, S, N = 2, 64, 32, 128, 1024, 512


def corner_matrix():
    eye = np.eye(DH)
    blk = np.block([[eye, eye], [-eye, eye]])
    return np.kron(np.eye(K), blk)


def setup_inputs():
    cen = np.random.uniform(-1.0, 1.0, (K, DH, S))
    mag = np.clip(0.5 + 0.1673 * np.random.standard_normal((K, DH, S)), 0.01, 0.99)
    sgn = np.where(np.random.random((K, DH, S)) < 0.5, -1.0, 1.0)
    table = np.concatenate([cen, mag * sgn], axis=1).reshape(F, S)
    return {"table": bf(table), "w": bf(corner_matrix()), "offs": striped(np.random.permutation(np.tile(np.arange(S), 2))[:N])}


def reference(table, w, offs):
    idx = offs[:16].T.reshape(-1)
    t = f64(table)
    is_off = (np.arange(F) % D >= DH)[:, None]
    tab = np.where(is_off, np.abs(t), t)
    return f64(w).T @ tab[:, idx]

@@ -1,0 +1,38 @@
+import concourse.mybir as mybir
+
+BF16 = mybir.dt.bfloat16
+F32 = mybir.dt.float32
+U16 = mybir.dt.uint16
+ABS = mybir.ActivationFunctionType.Abs
+
+F = 128
+HALF_BOX = 32
+S = 1024
+N = 512
+
+FLOPS = 2 * F * F * N
+
+
+def tile_multiboxel_kernel(tc, table, w, offs, out):
+    nc = tc.nc
+    with (
+        tc.tile_pool(name="held", bufs=1) as held,
+        tc.psum_pool(name="psum", bufs=1) as psum,
+    ):
+        offsets = held.tile([F, N // 16], U16, name="offsets")
+        nc.sync.dma_start(offsets[:], offs)
+        tab = held.tile([F, S], BF16, name="tab")
+        nc.sync.dma_start(tab[:], table)
+        weights = held.tile([F, F], BF16, name="weights")
+        nc.sync.dma_start(weights[:], w)
+
+        for first_offset_row in (HALF_BOX, 3 * HALF_BOX):
+            offset_rows = tab[first_offset_row : first_offset_row + HALF_BOX, :]
+            nc.scalar.activation(offset_rows, offset_rows, ABS)
+
+        corners = psum.tile([F, N], F32, name="corners")
+        nc.tensor.matmul(corners[:], weights[:], tab[:].indirect(offsets[:]), start=True, stop=True)
+
+        staged = held.tile([F, N], F32, name="staged")
+        nc.vector.tensor_copy(staged[:], corners[:])
+        nc.sync.dma_start(out, staged[:])

@@ -2,13 +2,17 @@ import concourse.mybir as mybir
 
 BF16 = mybir.dt.bfloat16
 F32 = mybir.dt.float32
+I32 = mybir.dt.int32
 U16 = mybir.dt.uint16
-ABS = mybir.ActivationFunctionType.Abs
+AND = mybir.AluOpType.bitwise_and
 
 F = 128
 HALF_BOX = 32
 S = 1024
 N = 512
+
+KEEP_ALL = -1
+CLEAR_SIGNS = 0x7FFF7FFF
 
 FLOPS = 2 * F * F * N
 
@@ -21,14 +25,18 @@ def tile_multiboxel_kernel(tc, table, w, offs, out):
     ):
         offsets = held.tile([F, N // 16], U16, name="offsets")
         nc.sync.dma_start(offsets[:], offs)
-        tab = held.tile([F, S], BF16, name="tab")
-        nc.sync.dma_start(tab[:], table)
+        raw = held.tile([F, S], BF16, name="raw")
+        nc.sync.dma_start(raw[:], table)
         weights = held.tile([F, F], BF16, name="weights")
         nc.sync.dma_start(weights[:], w)
 
-        for first_offset_row in (HALF_BOX, 3 * HALF_BOX):
-            offset_rows = tab[first_offset_row : first_offset_row + HALF_BOX, :]
-            nc.scalar.activation(offset_rows, offset_rows, ABS)
+        mask = held.tile([F, 1], I32, name="mask")
+        for block in range(F // HALF_BOX):
+            rows = mask[block * HALF_BOX : (block + 1) * HALF_BOX, :]
+            nc.vector.memset(rows, CLEAR_SIGNS if block % 2 else KEEP_ALL)
+
+        tab = held.tile([F, S], BF16, name="tab")
+        nc.vector.tensor_scalar(tab[:].bitcast(I32), raw[:].bitcast(I32), mask[:, 0:1], None, AND)
 
         corners = psum.tile([F, N], F32, name="corners")
         nc.tensor.matmul(corners[:], weights[:], tab[:].indirect(offsets[:]), start=True, stop=True)

@@ -16,6 +16,9 @@ CLEAR_SIGNS = 0x7FFF7FFF
 
 FLOPS = 2 * F * F * N
 
+PIECES = 2
+PIECE = N // PIECES
+
 
 def tile_multiboxel_kernel(tc, table, w, offs, out):
     nc = tc.nc
@@ -38,9 +41,11 @@ def tile_multiboxel_kernel(tc, table, w, offs, out):
         tab = held.tile([F, S], BF16, name="tab")
         nc.vector.tensor_scalar(tab[:].bitcast(I32), raw[:].bitcast(I32), mask[:, 0:1], None, AND)
 
-        corners = psum.tile([F, N], F32, name="corners")
-        nc.tensor.matmul(corners[:], weights[:], tab[:].indirect(offsets[:]), start=True, stop=True)
-
-        staged = held.tile([F, N], F32, name="staged")
-        nc.vector.tensor_copy(staged[:], corners[:])
-        nc.sync.dma_start(out, staged[:])
+        store_queues = (nc.sync, nc.scalar)
+        for piece in range(PIECES):
+            piece_offsets = offsets[:, piece * (PIECE // 16) : (piece + 1) * (PIECE // 16)]
+            corners = psum.tile([F, PIECE], F32, name=f"corners{piece}")
+            nc.tensor.matmul(corners[:], weights[:], tab[:].indirect(piece_offsets), start=True, stop=True)
+            staged = held.tile([F, PIECE], F32, name=f"staged{piece}")
+            nc.vector.tensor_copy(staged[:], corners[:])
+            store_queues[piece % 2].dma_start(out[:, piece * PIECE : (piece + 1) * PIECE], staged[:])

@@ -18,6 +18,7 @@ FLOPS = 2 * F * F * N
 
 PIECES = 2
 PIECE = N // PIECES
+WARM_UP_MATMULS = 5
 
 
 def tile_multiboxel_kernel(tc, table, w, offs, out):
@@ -32,6 +33,12 @@ def tile_multiboxel_kernel(tc, table, w, offs, out):
         nc.sync.dma_start(raw[:], table)
         weights = held.tile([F, F], BF16, name="weights")
         nc.sync.dma_start(weights[:], w)
+
+        zeros = held.tile([F, N], BF16, name="zeros")
+        nc.vector.memset(zeros[:].bitcast(I32), 0)
+        unused = psum.tile([F, N], F32, name="unused")
+        for step in range(WARM_UP_MATMULS):
+            nc.tensor.matmul(unused[:], zeros[:, 0:F], zeros[:], start=True, stop=True)
 
         mask = held.tile([F, 1], I32, name="mask")
         for block in range(F // HALF_BOX):

@@ -18,7 +18,8 @@ FLOPS = 2 * F * F * N
 
 PIECES = 2
 PIECE = N // PIECES
-WARM_UP_MATMULS = 5
+LOADS = 2
+LOAD = S // LOADS
 
 
 def tile_multiboxel_kernel(tc, table, w, offs, out):
@@ -27,18 +28,13 @@ def tile_multiboxel_kernel(tc, table, w, offs, out):
         tc.tile_pool(name="held", bufs=1) as held,
         tc.psum_pool(name="psum", bufs=1) as psum,
     ):
+        raw = held.tile([F, S], BF16, name="raw")
+        for load in range(LOADS):
+            nc.scalar.dma_start(raw[:, load * LOAD : (load + 1) * LOAD], table[:, load * LOAD : (load + 1) * LOAD])
         offsets = held.tile([F, N // 16], U16, name="offsets")
         nc.sync.dma_start(offsets[:], offs)
-        raw = held.tile([F, S], BF16, name="raw")
-        nc.sync.dma_start(raw[:], table)
         weights = held.tile([F, F], BF16, name="weights")
         nc.sync.dma_start(weights[:], w)
-
-        zeros = held.tile([F, N], BF16, name="zeros")
-        nc.vector.memset(zeros[:].bitcast(I32), 0)
-        unused = psum.tile([F, N], F32, name="unused")
-        for step in range(WARM_UP_MATMULS):
-            nc.tensor.matmul(unused[:], zeros[:, 0:F], zeros[:], start=True, stop=True)
 
         mask = held.tile([F, 1], I32, name="mask")
         for block in range(F // HALF_BOX):
@@ -46,7 +42,14 @@ def tile_multiboxel_kernel(tc, table, w, offs, out):
             nc.vector.memset(rows, CLEAR_SIGNS if block % 2 else KEEP_ALL)
 
         tab = held.tile([F, S], BF16, name="tab")
-        nc.vector.tensor_scalar(tab[:].bitcast(I32), raw[:].bitcast(I32), mask[:, 0:1], None, AND)
+        for load in range(LOADS):
+            nc.vector.tensor_scalar(
+                tab[:, load * LOAD : (load + 1) * LOAD].bitcast(I32),
+                raw[:, load * LOAD : (load + 1) * LOAD].bitcast(I32),
+                mask[:, 0:1],
+                None,
+                AND,
+            )
 
         store_queues = (nc.sync, nc.scalar)
         for piece in range(PIECES):

@@ -18,8 +18,6 @@ FLOPS = 2 * F * F * N
 
 PIECES = 2
 PIECE = N // PIECES
-LOADS = 2
-LOAD = S // LOADS
 
 
 def tile_multiboxel_kernel(tc, table, w, offs, out):
@@ -28,11 +26,10 @@ def tile_multiboxel_kernel(tc, table, w, offs, out):
         tc.tile_pool(name="held", bufs=1) as held,
         tc.psum_pool(name="psum", bufs=1) as psum,
     ):
-        raw = held.tile([F, S], BF16, name="raw")
-        for load in range(LOADS):
-            nc.scalar.dma_start(raw[:, load * LOAD : (load + 1) * LOAD], table[:, load * LOAD : (load + 1) * LOAD])
         offsets = held.tile([F, N // 16], U16, name="offsets")
         nc.sync.dma_start(offsets[:], offs)
+        raw = held.tile([F, S], BF16, name="raw")
+        nc.sync.dma_start(raw[:], table)
         weights = held.tile([F, F], BF16, name="weights")
         nc.sync.dma_start(weights[:], w)
 
@@ -42,20 +39,12 @@ def tile_multiboxel_kernel(tc, table, w, offs, out):
             nc.vector.memset(rows, CLEAR_SIGNS if block % 2 else KEEP_ALL)
 
         tab = held.tile([F, S], BF16, name="tab")
-        for load in range(LOADS):
-            nc.vector.tensor_scalar(
-                tab[:, load * LOAD : (load + 1) * LOAD].bitcast(I32),
-                raw[:, load * LOAD : (load + 1) * LOAD].bitcast(I32),
-                mask[:, 0:1],
-                None,
-                AND,
-            )
+        nc.vector.tensor_scalar(tab[:].bitcast(I32), raw[:].bitcast(I32), mask[:, 0:1], None, AND)
 
-        store_queues = (nc.sync, nc.scalar)
         for piece in range(PIECES):
             piece_offsets = offsets[:, piece * (PIECE // 16) : (piece + 1) * (PIECE // 16)]
             corners = psum.tile([F, PIECE], F32, name=f"corners{piece}")
             nc.tensor.matmul(corners[:], weights[:], tab[:].indirect(piece_offsets), start=True, stop=True)
             staged = held.tile([F, PIECE], F32, name=f"staged{piece}")
             nc.vector.tensor_copy(staged[:], corners[:])
-            store_queues[piece % 2].dma_start(out[:, piece * PIECE : (piece + 1) * PIECE], staged[:])
+            nc.sync.dma_start(out[:, piece * PIECE : (piece + 1) * PIECE], staged[:])

@@ -26,10 +26,10 @@ def tile_multiboxel_kernel(tc, table, w, offs, out):
         tc.tile_pool(name="held", bufs=1) as held,
         tc.psum_pool(name="psum", bufs=1) as psum,
     ):
-        offsets = held.tile([F, N // 16], U16, name="offsets")
-        nc.sync.dma_start(offsets[:], offs)
         raw = held.tile([F, S], BF16, name="raw")
         nc.sync.dma_start(raw[:], table)
+        offsets = held.tile([F, N // 16], U16, name="offsets")
+        nc.sync.dma_start(offsets[:], offs)
         weights = held.tile([F, F], BF16, name="weights")
         nc.sync.dma_start(weights[:], w)
 

@@ -18,6 +18,8 @@ FLOPS = 2 * F * F * N
 
 PIECES = 2
 PIECE = N // PIECES
+LOADS = 2
+LOAD = S // LOADS
 
 
 def tile_multiboxel_kernel(tc, table, w, offs, out):
@@ -27,7 +29,8 @@ def tile_multiboxel_kernel(tc, table, w, offs, out):
         tc.psum_pool(name="psum", bufs=1) as psum,
     ):
         raw = held.tile([F, S], BF16, name="raw")
-        nc.sync.dma_start(raw[:], table)
+        for load in range(LOADS):
+            nc.sync.dma_start(raw[:, load * LOAD : (load + 1) * LOAD], table[:, load * LOAD : (load + 1) * LOAD])
         offsets = held.tile([F, N // 16], U16, name="offsets")
         nc.sync.dma_start(offsets[:], offs)
         weights = held.tile([F, F], BF16, name="weights")
@@ -39,7 +42,14 @@ def tile_multiboxel_kernel(tc, table, w, offs, out):
             nc.vector.memset(rows, CLEAR_SIGNS if block % 2 else KEEP_ALL)
 
         tab = held.tile([F, S], BF16, name="tab")
-        nc.vector.tensor_scalar(tab[:].bitcast(I32), raw[:].bitcast(I32), mask[:, 0:1], None, AND)
+        for load in range(LOADS):
+            nc.vector.tensor_scalar(
+                tab[:, load * LOAD : (load + 1) * LOAD].bitcast(I32),
+                raw[:, load * LOAD : (load + 1) * LOAD].bitcast(I32),
+                mask[:, 0:1],
+                None,
+                AND,
+            )
 
         for piece in range(PIECES):
             piece_offsets = offsets[:, piece * (PIECE // 16) : (piece + 1) * (PIECE // 16)]

@@ -16,8 +16,9 @@ CLEAR_SIGNS = 0x7FFF7FFF
 
 FLOPS = 2 * F * F * N
 
-PIECES = 2
+PIECES = 4
 PIECE = N // PIECES
+BANK = 512
 LOADS = 2
 LOAD = S // LOADS
 
@@ -53,8 +54,8 @@ def tile_multiboxel_kernel(tc, table, w, offs, out):
 
         for piece in range(PIECES):
             piece_offsets = offsets[:, piece * (PIECE // 16) : (piece + 1) * (PIECE // 16)]
-            corners = psum.tile([F, PIECE], F32, name=f"corners{piece}")
-            nc.tensor.matmul(corners[:], weights[:], tab[:].indirect(piece_offsets), start=True, stop=True)
+            corners = psum.tile([F, BANK], F32, name=f"corners{piece}")
+            nc.tensor.matmul(corners[:, 0:PIECE], weights[:], tab[:].indirect(piece_offsets), start=True, stop=True)
             staged = held.tile([F, PIECE], F32, name=f"staged{piece}")
-            nc.vector.tensor_copy(staged[:], corners[:])
+            nc.vector.tensor_copy(staged[:], corners[:, 0:PIECE])
             nc.sync.dma_start(out[:, piece * PIECE : (piece + 1) * PIECE], staged[:])

@@ -19,6 +19,7 @@ FLOPS = 2 * F * F * N
 PIECES = 4
 PIECE = N // PIECES
 BANK = 512
+BURST = 256
 LOADS = 2
 LOAD = S // LOADS
 
@@ -29,12 +30,12 @@ def tile_multiboxel_kernel(tc, table, w, offs, out):
         tc.tile_pool(name="held", bufs=1) as held,
         tc.psum_pool(name="psum", bufs=1) as psum,
     ):
-        raw = held.tile([F, S], BF16, name="raw")
+        raw = held.tile([F, S], BF16, name="raw", align_bytes=BURST)
         for load in range(LOADS):
             nc.sync.dma_start(raw[:, load * LOAD : (load + 1) * LOAD], table[:, load * LOAD : (load + 1) * LOAD])
         offsets = held.tile([F, N // 16], U16, name="offsets")
         nc.sync.dma_start(offsets[:], offs)
-        weights = held.tile([F, F], BF16, name="weights")
+        weights = held.tile([F, F], BF16, name="weights", align_bytes=BURST)
         nc.sync.dma_start(weights[:], w)
 
         mask = held.tile([F, 1], I32, name="mask")
@@ -56,6 +57,6 @@ def tile_multiboxel_kernel(tc, table, w, offs, out):
             piece_offsets = offsets[:, piece * (PIECE // 16) : (piece + 1) * (PIECE // 16)]
             corners = psum.tile([F, BANK], F32, name=f"corners{piece}")
             nc.tensor.matmul(corners[:, 0:PIECE], weights[:], tab[:].indirect(piece_offsets), start=True, stop=True)
-            staged = held.tile([F, PIECE], F32, name=f"staged{piece}")
+            staged = held.tile([F, PIECE], F32, name=f"staged{piece}", align_bytes=BURST)
             nc.vector.tensor_copy(staged[:], corners[:, 0:PIECE])
             nc.sync.dma_start(out[:, piece * PIECE : (piece + 1) * PIECE], staged[:])

@@ -20,6 +20,9 @@ PIECES = 4
 PIECE = N // PIECES
 BANK = 512
 BURST = 256
+LOAD_ROW = 2 * (S // 2)
+WEIGHT_ROW = 2 * F
+STORE_ROW = 4 * PIECE
 LOADS = 2
 LOAD = S // LOADS
 
@@ -30,12 +33,12 @@ def tile_multiboxel_kernel(tc, table, w, offs, out):
         tc.tile_pool(name="held", bufs=1) as held,
         tc.psum_pool(name="psum", bufs=1) as psum,
     ):
-        raw = held.tile([F, S], BF16, name="raw", align_bytes=BURST)
+        raw = held.tile([F, S], BF16, name="raw", align_bytes=LOAD_ROW)
         for load in range(LOADS):
             nc.sync.dma_start(raw[:, load * LOAD : (load + 1) * LOAD], table[:, load * LOAD : (load + 1) * LOAD])
-        offsets = held.tile([F, N // 16], U16, name="offsets")
+        offsets = held.tile([F, N // 16], U16, name="offsets", align_bytes=BURST)
         nc.sync.dma_start(offsets[:], offs)
-        weights = held.tile([F, F], BF16, name="weights", align_bytes=BURST)
+        weights = held.tile([F, F], BF16, name="weights", align_bytes=WEIGHT_ROW)
         nc.sync.dma_start(weights[:], w)
 
         mask = held.tile([F, 1], I32, name="mask")
@@ -57,6 +60,6 @@ def tile_multiboxel_kernel(tc, table, w, offs, out):
             piece_offsets = offsets[:, piece * (PIECE // 16) : (piece + 1) * (PIECE // 16)]
             corners = psum.tile([F, BANK], F32, name=f"corners{piece}")
             nc.tensor.matmul(corners[:, 0:PIECE], weights[:], tab[:].indirect(piece_offsets), start=True, stop=True)
-            staged = held.tile([F, PIECE], F32, name=f"staged{piece}", align_bytes=BURST)
+            staged = held.tile([F, PIECE], F32, name=f"staged{piece}", align_bytes=STORE_ROW)
             nc.vector.tensor_copy(staged[:], corners[:, 0:PIECE])
             nc.sync.dma_start(out[:, piece * PIECE : (piece + 1) * PIECE], staged[:])

@@ -17,12 +17,14 @@ CLEAR_SIGNS = 0x7FFF7FFF
 FLOPS = 2 * F * F * N
 
 PIECES = 4
+STORES = 2
 PIECE = N // PIECES
 BANK = 512
 BURST = 256
 LOAD_ROW = 2 * (S // 2)
 WEIGHT_ROW = 2 * F
-STORE_ROW = 4 * PIECE
+STORE = N // STORES
+STORE_ROW = 4 * STORE
 LOADS = 2
 LOAD = S // LOADS
 
@@ -56,10 +58,12 @@ def tile_multiboxel_kernel(tc, table, w, offs, out):
                 AND,
             )
 
-        for piece in range(PIECES):
-            piece_offsets = offsets[:, piece * (PIECE // 16) : (piece + 1) * (PIECE // 16)]
-            corners = psum.tile([F, BANK], F32, name=f"corners{piece}")
-            nc.tensor.matmul(corners[:, 0:PIECE], weights[:], tab[:].indirect(piece_offsets), start=True, stop=True)
-            staged = held.tile([F, PIECE], F32, name=f"staged{piece}", align_bytes=STORE_ROW)
-            nc.vector.tensor_copy(staged[:], corners[:, 0:PIECE])
-            nc.sync.dma_start(out[:, piece * PIECE : (piece + 1) * PIECE], staged[:])
+        for store in range(STORES):
+            staged = held.tile([F, STORE], F32, name=f"staged{store}", align_bytes=STORE_ROW)
+            for part in range(PIECES // STORES):
+                piece = store * (PIECES // STORES) + part
+                piece_offsets = offsets[:, piece * (PIECE // 16) : (piece + 1) * (PIECE // 16)]
+                corners = psum.tile([F, BANK], F32, name=f"corners{piece}")
+                nc.tensor.matmul(corners[:, 0:PIECE], weights[:], tab[:].indirect(piece_offsets), start=True, stop=True)
+                nc.vector.tensor_copy(staged[:, part * PIECE : (part + 1) * PIECE], corners[:, 0:PIECE])
+            nc.sync.dma_start(out[:, store * STORE : (store + 1) * STORE], staged[:])

import concourse.mybir as mybir

BF16 = mybir.dt.bfloat16
F32 = mybir.dt.float32
I32 = mybir.dt.int32
U16 = mybir.dt.uint16
AND = mybir.AluOpType.bitwise_and

F = 128
HALF_BOX = 32
S = 1024
N = 512

KEEP_ALL = -1
CLEAR_SIGNS = 0x7FFF7FFF

FLOPS = 2 * F * F * N

PIECES = 4
STORES = 2
PIECE = N // PIECES
BANK = 512
BURST = 256
LOAD_ROW = 2 * (S // 2)
WEIGHT_ROW = 2 * F
STORE = N // STORES
STORE_ROW = 4 * STORE
LOADS = 2
LOAD = S // LOADS


def tile_multiboxel_kernel(tc, table, w, offs, out):
    nc = tc.nc
    with (
        tc.tile_pool(name="held", bufs=1) as held,
        tc.psum_pool(name="psum", bufs=1) as psum,
    ):
        raw = held.tile([F, S], BF16, name="raw", align_bytes=LOAD_ROW)
        for load in range(LOADS):
            nc.sync.dma_start(raw[:, load * LOAD : (load + 1) * LOAD], table[:, load * LOAD : (load + 1) * LOAD])
        offsets = held.tile([F, N // 16], U16, name="offsets", align_bytes=BURST)
        nc.sync.dma_start(offsets[:], offs)
        weights = held.tile([F, F], BF16, name="weights", align_bytes=WEIGHT_ROW)
        nc.sync.dma_start(weights[:], w)

        mask = held.tile([F, 1], I32, name="mask")
        for block in range(F // HALF_BOX):
            rows = mask[block * HALF_BOX : (block + 1) * HALF_BOX, :]
            nc.vector.memset(rows, CLEAR_SIGNS if block % 2 else KEEP_ALL)

        tab = held.tile([F, S], BF16, name="tab")
        for load in range(LOADS):
            nc.vector.tensor_scalar(
                tab[:, load * LOAD : (load + 1) * LOAD].bitcast(I32),
                raw[:, load * LOAD : (load + 1) * LOAD].bitcast(I32),
                mask[:, 0:1],
                None,
                AND,
            )

        for store in range(STORES):
            staged = held.tile([F, STORE], F32, name=f"staged{store}", align_bytes=STORE_ROW)
            for part in range(PIECES // STORES):
                piece = store * (PIECES // STORES) + part
                piece_offsets = offsets[:, piece * (PIECE // 16) : (piece + 1) * (PIECE // 16)]
                corners = psum.tile([F, BANK], F32, name=f"corners{piece}")
                nc.tensor.matmul(corners[:, 0:PIECE], weights[:], tab[:].indirect(piece_offsets), start=True, stop=True)
                nc.vector.tensor_copy(staged[:, part * PIECE : (part + 1) * PIECE], corners[:, 0:PIECE])
            nc.sync.dma_start(out[:, store * STORE : (store + 1) * STORE], staged[:])
